import numpy as np
import ml_dtypes

BF16 = ml_dtypes.bfloat16


def bf(x):
    return np.asarray(x, np.float32).astype(BF16)


def f32(x):
    return np.asarray(x, np.float32)


def f64(x):
    return np.asarray(x).astype(np.float64)


def striped(idx):
    return np.tile(idx.reshape(-1, 16).T, (8, 1))


K, C, CIN, S, N = 4, 128, 256, 256, 1024
E = 0.01
BN_EPS = 1e-5
POOL = 0.25
LO, HI = 0.2, 1.2


def stab(z):
    return z + np.where(z >= 0, E, -E)


def away(shape):
    return np.random.uniform(LO, HI, shape) * np.where(np.random.random(shape) < 0.5, -1.0, 1.0)


def setup_inputs():
    return {
        "r_stack": f32(np.random.standard_normal((K, C, S))),
        "a_stack": f32(away((K, C, S))),
        "gamma": f32(np.random.uniform(0.5, 1.5, (C, K))),
        "var": f32(np.random.uniform(0.5, 1.5, (C, K))),
        "a_pool": f32(np.random.standard_normal((C, S))),
        "aj_pool": f32(np.random.uniform(0.0, 1.0, (C, N))),
        "a_conv": f32(away((C, N))),
        "aj_conv": f32(np.random.uniform(0.0, 1.0, (CIN, N))),
        "w_conv": bf(0.05 * np.random.standard_normal((C, CIN))),
        "offs": striped(np.concatenate([np.random.permutation(S) for _ in range(-(-(N) // S))])[:N]),
    }


def reference(r_stack, a_stack, gamma, var, a_pool, aj_pool, a_conv, aj_conv, w_conv, offs):
    idx = offs[:16].T.reshape(-1)
    wbn = f64(gamma) / np.sqrt(f64(var) + BN_EPS)
    s_total = np.sum(f64(r_stack) / stab(f64(a_stack)) * wbn.T[:, :, None], axis=0)
    s_pool = f64(a_pool) * s_total / stab(f64(a_pool))
    r = s_pool[:, idx] * f64(aj_pool) * POOL
    sc = r / stab(f64(a_conv))
    return f64(aj_conv) * (f64(w_conv).T @ sc)

@@ -1,0 +1,126 @@
+import concourse.mybir as mybir
+from concourse.masks import make_identity
+
+F32 = mybir.dt.float32
+BF16 = mybir.dt.bfloat16
+U16 = mybir.dt.uint16
+ALU = mybir.AluOpType
+ACT = mybir.ActivationFunctionType
+
+P = 128
+K = 4
+S = 256
+N = 1024
+MB = 2
+PIECE = 256
+NPIECES = N // PIECE
+E = 0.01
+BN_EPS = 1e-5
+POOL = 0.25
+
+FLOPS = 2 * P * MB * P * N
+
+
+def inverse_magnitude(nc, out, scratch, z):
+    nc.scalar.activation(scratch, z, ACT.Abs)
+    nc.scalar.activation(scratch, scratch, ACT.Abs_reciprocal_sqrt, bias=E)
+    nc.scalar.activation(out, scratch, ACT.Square)
+
+
+def half_sign(nc, out, z):
+    nc.vector.tensor_scalar(out, z, 0.0, 0.5, ALU.is_ge, ALU.subtract)
+
+
+def tile_lrpdensenettransition_kernel(
+    tc, r_stack, a_stack, gamma, var, a_pool, aj_pool, a_conv, aj_conv, w_conv, offs, out
+):
+    nc = tc.nc
+    with (
+        tc.tile_pool(name="held", bufs=1) as held,
+        tc.psum_pool(name="psum_total", bufs=1) as psum_total,
+        tc.psum_pool(name="psum_conv", bufs=NPIECES) as psum_conv,
+    ):
+        offsets = held.tile([P, N // 16], U16, name="offsets")
+        nc.sync.dma_start(offsets[:], offs)
+        var_t = held.tile([P, K], F32)
+        nc.scalar.dma_start(var_t[:], var)
+        gamma_t = held.tile([P, K], F32)
+        nc.scalar.dma_start(gamma_t[:], gamma)
+        a_st = held.tile([P, K, S], F32)
+        r_st = held.tile([P, K, S], F32)
+        for k in range(K):
+            nc.sync.dma_start(a_st[:, k, :], a_stack[k])
+        a_pl = held.tile([P, S], F32)
+        nc.scalar.dma_start(a_pl[:], a_pool)
+        for k in range(K):
+            nc.scalar.dma_start(r_st[:, k, :], r_stack[k])
+        a_cv = held.tile([P, N], F32)
+        nc.sync.dma_start(a_cv[:], a_conv)
+        aj_pl = held.tile([P, N], F32)
+        nc.scalar.dma_start(aj_pl[:], aj_pool)
+        w_t = held.tile([P, MB * P], BF16)
+        nc.sync.dma_start(w_t[:], w_conv)
+        aj_cv = held.tile([P, MB, N], F32)
+        nc.sync.dma_start(aj_cv[:, 0, :], aj_conv[0:P, :])
+        nc.scalar.dma_start(aj_cv[:, 1, :], aj_conv[P : 2 * P, :])
+
+        identity = held.tile([P, P], F32)
+        make_identity(nc, identity[:])
+
+        rstd = held.tile([P, K], F32)
+        nc.scalar.activation(rstd[:], var_t[:], ACT.Abs_reciprocal_sqrt, bias=BN_EPS)
+        wbn2 = held.tile([P, K], F32)
+        nc.vector.scalar_tensor_tensor(wbn2[:], gamma_t[:], 2.0, rstd[:], ALU.mult, ALU.mult)
+
+        mag_st = held.tile([P, K, S], F32)
+        inv_st = held.tile([P, K, S], F32)
+        sgn_st = held.tile([P, K, S], F32)
+        term = held.tile([P, K, S], F32)
+        s_total = psum_total.tile([P, S], F32)
+        for k in range(K):
+            inverse_magnitude(nc, inv_st[:, k, :], mag_st[:, k, :], a_st[:, k, :])
+            half_sign(nc, sgn_st[:, k, :], a_st[:, k, :])
+            nc.vector.scalar_tensor_tensor(
+                term[:, k, :], r_st[:, k, :], wbn2[:, k : k + 1], sgn_st[:, k, :], ALU.mult, ALU.mult
+            )
+            nc.vector.tensor_tensor(term[:, k, :], term[:, k, :], inv_st[:, k, :], ALU.mult)
+            nc.tensor.matmul(s_total[:], identity[:], term[:, k, :], start=(k == 0), stop=(k == K - 1))
+
+        mag_pl = held.tile([P, S], F32)
+        nc.scalar.activation(mag_pl[:], a_pl[:], ACT.Abs)
+        inv_pl = held.tile([P, S], F32)
+        nc.scalar.activation(inv_pl[:], mag_pl[:], ACT.Abs_reciprocal_sqrt, bias=E)
+        nc.scalar.activation(inv_pl[:], inv_pl[:], ACT.Square)
+        share = held.tile([P, S], F32)
+        nc.vector.tensor_tensor(share[:], mag_pl[:], inv_pl[:], ALU.mult)
+        s_pool = held.tile([P, S], F32)
+        nc.vector.tensor_tensor(s_pool[:], s_total[:], share[:], ALU.mult)
+
+        sgn_cv = held.tile([P, N], F32)
+        half_sign(nc, sgn_cv[:], a_cv[:])
+        aj_signed = held.tile([P, N], F32)
+        nc.vector.tensor_tensor(aj_signed[:], aj_pl[:], sgn_cv[:], ALU.mult)
+        mag_cv = held.tile([P, N], F32)
+        inv_cv = held.tile([P, N], F32)
+
+        picked = held.tile([P, N], F32)
+        sc = held.tile([P, N], BF16)
+        result = held.tile([P, MB, N], F32)
+        out_blocks = out.rearrange("(b p) j -> p b j", p=P)
+        for i in range(NPIECES):
+            cols = slice(i * PIECE, (i + 1) * PIECE)
+            inverse_magnitude(nc, inv_cv[:, cols], mag_cv[:, cols], a_cv[:, cols])
+            nc.vector.tensor_tensor(
+                picked[:, cols],
+                s_pool[:].indirect(offsets[:, i * (PIECE // 16) : (i + 1) * (PIECE // 16)]),
+                aj_signed[:, cols],
+                ALU.mult,
+            )
+            nc.vector.scalar_tensor_tensor(
+                sc[:, cols], picked[:, cols], 2.0 * POOL, inv_cv[:, cols], ALU.mult, ALU.mult
+            )
+            conv = psum_conv.tile([P, MB, PIECE], F32)
+            for b in range(MB):
+                nc.tensor.matmul(conv[:, b, :], w_t[:, b * P : (b + 1) * P], sc[:, cols], start=True, stop=True)
+            nc.vector.tensor_tensor(result[:, :, cols], conv[:], aj_cv[:, :, cols], ALU.mult)
+            nc.sync.dma_start(out_blocks[:, :, cols], result[:, :, cols])

@@ -1,8 +1,8 @@
 import concourse.mybir as mybir
-from concourse.masks import make_identity
 
 F32 = mybir.dt.float32
 BF16 = mybir.dt.bfloat16
+I32 = mybir.dt.int32
 U16 = mybir.dt.uint16
 ALU = mybir.AluOpType
 ACT = mybir.ActivationFunctionType
@@ -17,14 +17,18 @@ NPIECES = N // PIECE
 E = 0.01
 BN_EPS = 1e-5
 POOL = 0.25
+ALL_BUT_SIGN = 0x7FFFFFFF
 
 FLOPS = 2 * P * MB * P * N
 
 
-def inverse_magnitude(nc, out, scratch, z):
-    nc.scalar.activation(scratch, z, ACT.Abs)
-    nc.scalar.activation(scratch, scratch, ACT.Abs_reciprocal_sqrt, bias=E)
-    nc.scalar.activation(out, scratch, ACT.Square)
+def magnitude(nc, out, z):
+    nc.vector.tensor_scalar(out.bitcast(I32), z.bitcast(I32), ALL_BUT_SIGN, None, ALU.bitwise_and)
+
+
+def inverse_of_stabilised(nc, out, mag):
+    nc.scalar.activation(out, mag, ACT.Abs_reciprocal_sqrt, bias=E)
+    nc.scalar.activation(out, out, ACT.Square)
 
 
 def half_sign(nc, out, z):
@@ -37,35 +41,29 @@ def tile_lrpdensenettransition_kernel(
     nc = tc.nc
     with (
         tc.tile_pool(name="held", bufs=1) as held,
-        tc.psum_pool(name="psum_total", bufs=1) as psum_total,
         tc.psum_pool(name="psum_conv", bufs=NPIECES) as psum_conv,
     ):
-        offsets = held.tile([P, N // 16], U16, name="offsets")
-        nc.sync.dma_start(offsets[:], offs)
         var_t = held.tile([P, K], F32)
         nc.scalar.dma_start(var_t[:], var)
         gamma_t = held.tile([P, K], F32)
         nc.scalar.dma_start(gamma_t[:], gamma)
+        w_t = held.tile([P, MB * P], BF16)
+        nc.scalar.dma_start(w_t[:], w_conv)
         a_st = held.tile([P, K, S], F32)
+        for k in range(0, K, 2):
+            nc.sync.dma_start(a_st[:, k : k + 2, :], a_stack[k : k + 2].rearrange("k c s -> c k s"))
         r_st = held.tile([P, K, S], F32)
-        for k in range(K):
-            nc.sync.dma_start(a_st[:, k, :], a_stack[k])
+        nc.sync.dma_start(r_st[:], r_stack.rearrange("k c s -> c k s"))
         a_pl = held.tile([P, S], F32)
-        nc.scalar.dma_start(a_pl[:], a_pool)
-        for k in range(K):
-            nc.scalar.dma_start(r_st[:, k, :], r_stack[k])
+        nc.sync.dma_start(a_pl[:], a_pool)
         a_cv = held.tile([P, N], F32)
         nc.sync.dma_start(a_cv[:], a_conv)
         aj_pl = held.tile([P, N], F32)
-        nc.scalar.dma_start(aj_pl[:], aj_pool)
-        w_t = held.tile([P, MB * P], BF16)
-        nc.sync.dma_start(w_t[:], w_conv)
+        nc.sync.dma_start(aj_pl[:], aj_pool)
+        offsets = held.tile([P, N // 16], U16, name="offsets")
+        nc.sync.dma_start(offsets[:], offs)
         aj_cv = held.tile([P, MB, N], F32)
-        nc.sync.dma_start(aj_cv[:, 0, :], aj_conv[0:P, :])
-        nc.scalar.dma_start(aj_cv[:, 1, :], aj_conv[P : 2 * P, :])
-
-        identity = held.tile([P, P], F32)
-        make_identity(nc, identity[:])
+        nc.sync.dma_start(aj_cv[:], aj_conv.rearrange("(b p) j -> p b j", p=P))
 
         rstd = held.tile([P, K], F32)
         nc.scalar.activation(rstd[:], var_t[:], ACT.Abs_reciprocal_sqrt, bias=BN_EPS)
@@ -76,49 +74,52 @@ def tile_lrpdensenettransition_kernel(
         inv_st = held.tile([P, K, S], F32)
         sgn_st = held.tile([P, K, S], F32)
         term = held.tile([P, K, S], F32)
-        s_total = psum_total.tile([P, S], F32)
+        s_total = held.tile([P, S], F32)
         for k in range(K):
-            inverse_magnitude(nc, inv_st[:, k, :], mag_st[:, k, :], a_st[:, k, :])
+            magnitude(nc, mag_st[:, k, :], a_st[:, k, :])
+            inverse_of_stabilised(nc, inv_st[:, k, :], mag_st[:, k, :])
             half_sign(nc, sgn_st[:, k, :], a_st[:, k, :])
+            nc.vector.tensor_tensor(inv_st[:, k, :], inv_st[:, k, :], sgn_st[:, k, :], ALU.mult)
+        for k in range(K):
+            summand = s_total[:] if k == 0 else term[:, k, :]
             nc.vector.scalar_tensor_tensor(
-                term[:, k, :], r_st[:, k, :], wbn2[:, k : k + 1], sgn_st[:, k, :], ALU.mult, ALU.mult
+                summand, r_st[:, k, :], wbn2[:, k : k + 1], inv_st[:, k, :], ALU.mult, ALU.mult
             )
-            nc.vector.tensor_tensor(term[:, k, :], term[:, k, :], inv_st[:, k, :], ALU.mult)
-            nc.tensor.matmul(s_total[:], identity[:], term[:, k, :], start=(k == 0), stop=(k == K - 1))
+            if k > 0:
+                nc.vector.tensor_tensor(s_total[:], s_total[:], summand, ALU.add)
 
         mag_pl = held.tile([P, S], F32)
-        nc.scalar.activation(mag_pl[:], a_pl[:], ACT.Abs)
+        magnitude(nc, mag_pl[:], a_pl[:])
         inv_pl = held.tile([P, S], F32)
-        nc.scalar.activation(inv_pl[:], mag_pl[:], ACT.Abs_reciprocal_sqrt, bias=E)
-        nc.scalar.activation(inv_pl[:], inv_pl[:], ACT.Square)
+        inverse_of_stabilised(nc, inv_pl[:], mag_pl[:])
         share = held.tile([P, S], F32)
         nc.vector.tensor_tensor(share[:], mag_pl[:], inv_pl[:], ALU.mult)
         s_pool = held.tile([P, S], F32)
         nc.vector.tensor_tensor(s_pool[:], s_total[:], share[:], ALU.mult)
 
-        sgn_cv = held.tile([P, N], F32)
-        half_sign(nc, sgn_cv[:], a_cv[:])
-        aj_signed = held.tile([P, N], F32)
-        nc.vector.tensor_tensor(aj_signed[:], aj_pl[:], sgn_cv[:], ALU.mult)
         mag_cv = held.tile([P, N], F32)
         inv_cv = held.tile([P, N], F32)
-
+        sgn_cv = held.tile([P, N], BF16)
         picked = held.tile([P, N], F32)
+        sc_mag = held.tile([P, N], BF16)
         sc = held.tile([P, N], BF16)
         result = held.tile([P, MB, N], F32)
         out_blocks = out.rearrange("(b p) j -> p b j", p=P)
         for i in range(NPIECES):
             cols = slice(i * PIECE, (i + 1) * PIECE)
-            inverse_magnitude(nc, inv_cv[:, cols], mag_cv[:, cols], a_cv[:, cols])
+            nc.scalar.activation(mag_cv[:, cols], a_cv[:, cols], ACT.Abs)
+            inverse_of_stabilised(nc, inv_cv[:, cols], mag_cv[:, cols])
+            half_sign(nc, sgn_cv[:, cols], a_cv[:, cols])
             nc.vector.tensor_tensor(
                 picked[:, cols],
                 s_pool[:].indirect(offsets[:, i * (PIECE // 16) : (i + 1) * (PIECE // 16)]),
-                aj_signed[:, cols],
+                aj_pl[:, cols],
                 ALU.mult,
             )
             nc.vector.scalar_tensor_tensor(
-                sc[:, cols], picked[:, cols], 2.0 * POOL, inv_cv[:, cols], ALU.mult, ALU.mult
+                sc_mag[:, cols], picked[:, cols], 2.0 * POOL, inv_cv[:, cols], ALU.mult, ALU.mult
             )
+            nc.vector.tensor_tensor(sc[:, cols], sc_mag[:, cols], sgn_cv[:, cols], ALU.mult)
             conv = psum_conv.tile([P, MB, PIECE], F32)
             for b in range(MB):
                 nc.tensor.matmul(conv[:, b, :], w_t[:, b * P : (b + 1) * P], sc[:, cols], start=True, stop=True)

@@ -35,6 +35,10 @@ def half_sign(nc, out, z):
     nc.vector.tensor_scalar(out, z, 0.0, 0.5, ALU.is_ge, ALU.subtract)
 
 
+def sign_of_stabilised(nc, out, z):
+    nc.scalar.activation(out, z, ACT.Sign, bias=2.0**-126, scale=2.0**24)
+
+
 def tile_lrpdensenettransition_kernel(
     tc, r_stack, a_stack, gamma, var, a_pool, aj_pool, a_conv, aj_conv, w_conv, offs, out
 ):
@@ -47,15 +51,16 @@ def tile_lrpdensenettransition_kernel(
         nc.scalar.dma_start(var_t[:], var)
         gamma_t = held.tile([P, K], F32)
         nc.scalar.dma_start(gamma_t[:], gamma)
+        a_pl = held.tile([P, S], F32)
+        nc.scalar.dma_start(a_pl[:], a_pool)
         w_t = held.tile([P, MB * P], BF16)
         nc.scalar.dma_start(w_t[:], w_conv)
         a_st = held.tile([P, K, S], F32)
         for k in range(0, K, 2):
             nc.sync.dma_start(a_st[:, k : k + 2, :], a_stack[k : k + 2].rearrange("k c s -> c k s"))
         r_st = held.tile([P, K, S], F32)
-        nc.sync.dma_start(r_st[:], r_stack.rearrange("k c s -> c k s"))
-        a_pl = held.tile([P, S], F32)
-        nc.sync.dma_start(a_pl[:], a_pool)
+        for k in range(0, K, 2):
+            nc.sync.dma_start(r_st[:, k : k + 2, :], r_stack[k : k + 2].rearrange("k c s -> c k s"))
         a_cv = held.tile([P, N], F32)
         nc.sync.dma_start(a_cv[:], a_conv)
         aj_pl = held.tile([P, N], F32)
@@ -79,12 +84,11 @@ def tile_lrpdensenettransition_kernel(
             magnitude(nc, mag_st[:, k, :], a_st[:, k, :])
             inverse_of_stabilised(nc, inv_st[:, k, :], mag_st[:, k, :])
             half_sign(nc, sgn_st[:, k, :], a_st[:, k, :])
-            nc.vector.tensor_tensor(inv_st[:, k, :], inv_st[:, k, :], sgn_st[:, k, :], ALU.mult)
-        for k in range(K):
-            summand = s_total[:] if k == 0 else term[:, k, :]
             nc.vector.scalar_tensor_tensor(
-                summand, r_st[:, k, :], wbn2[:, k : k + 1], inv_st[:, k, :], ALU.mult, ALU.mult
+                term[:, k, :], r_st[:, k, :], wbn2[:, k : k + 1], sgn_st[:, k, :], ALU.mult, ALU.mult
             )
+            summand = s_total[:] if k == 0 else term[:, k, :]
+            nc.vector.tensor_tensor(summand, term[:, k, :], inv_st[:, k, :], ALU.mult)
             if k > 0:
                 nc.vector.tensor_tensor(s_total[:], s_total[:], summand, ALU.add)
 
@@ -97,11 +101,16 @@ def tile_lrpdensenettransition_kernel(
         s_pool = held.tile([P, S], F32)
         nc.vector.tensor_tensor(s_pool[:], s_total[:], share[:], ALU.mult)
 
+        sgn_cv = held.tile([P, N], F32)
+        aj_signed = held.tile([P, N], F32)
+        for i in range(NPIECES):
+            cols = slice(i * PIECE, (i + 1) * PIECE)
+            sign_of_stabilised(nc, sgn_cv[:, cols], a_cv[:, cols])
+            nc.vector.tensor_tensor(aj_signed[:, cols], aj_pl[:, cols], sgn_cv[:, cols], ALU.mult)
+
         mag_cv = held.tile([P, N], F32)
         inv_cv = held.tile([P, N], F32)
-        sgn_cv = held.tile([P, N], BF16)
         picked = held.tile([P, N], F32)
-        sc_mag = held.tile([P, N], BF16)
         sc = held.tile([P, N], BF16)
         result = held.tile([P, MB, N], F32)
         out_blocks = out.rearrange("(b p) j -> p b j", p=P)
@@ -109,17 +118,15 @@ def tile_lrpdensenettransition_kernel(
             cols = slice(i * PIECE, (i + 1) * PIECE)
             nc.scalar.activation(mag_cv[:, cols], a_cv[:, cols], ACT.Abs)
             inverse_of_stabilised(nc, inv_cv[:, cols], mag_cv[:, cols])
-            half_sign(nc, sgn_cv[:, cols], a_cv[:, cols])
             nc.vector.tensor_tensor(
                 picked[:, cols],
                 s_pool[:].indirect(offsets[:, i * (PIECE // 16) : (i + 1) * (PIECE // 16)]),
-                aj_pl[:, cols],
+                aj_signed[:, cols],
                 ALU.mult,
             )
             nc.vector.scalar_tensor_tensor(
-                sc_mag[:, cols], picked[:, cols], 2.0 * POOL, inv_cv[:, cols], ALU.mult, ALU.mult
+                sc[:, cols], picked[:, cols], POOL, inv_cv[:, cols], ALU.mult, ALU.mult
             )
-            nc.vector.tensor_tensor(sc[:, cols], sc_mag[:, cols], sgn_cv[:, cols], ALU.mult)
             conv = psum_conv.tile([P, MB, PIECE], F32)
             for b in range(MB):
                 nc.tensor.matmul(conv[:, b, :], w_t[:, b * P : (b + 1) * P], sc[:, cols], start=True, stop=True)

@@ -48,25 +48,25 @@ def tile_lrpdensenettransition_kernel(
         tc.psum_pool(name="psum_conv", bufs=NPIECES) as psum_conv,
     ):
         var_t = held.tile([P, K], F32)
-        nc.scalar.dma_start(var_t[:], var)
+        nc.sync.dma_start(var_t[:], var)
         gamma_t = held.tile([P, K], F32)
-        nc.scalar.dma_start(gamma_t[:], gamma)
-        a_pl = held.tile([P, S], F32)
-        nc.scalar.dma_start(a_pl[:], a_pool)
-        w_t = held.tile([P, MB * P], BF16)
-        nc.scalar.dma_start(w_t[:], w_conv)
+        nc.sync.dma_start(gamma_t[:], gamma)
         a_st = held.tile([P, K, S], F32)
         for k in range(0, K, 2):
             nc.sync.dma_start(a_st[:, k : k + 2, :], a_stack[k : k + 2].rearrange("k c s -> c k s"))
         r_st = held.tile([P, K, S], F32)
         for k in range(0, K, 2):
             nc.sync.dma_start(r_st[:, k : k + 2, :], r_stack[k : k + 2].rearrange("k c s -> c k s"))
+        a_pl = held.tile([P, S], F32)
+        nc.sync.dma_start(a_pl[:], a_pool)
         a_cv = held.tile([P, N], F32)
         nc.sync.dma_start(a_cv[:], a_conv)
         aj_pl = held.tile([P, N], F32)
         nc.sync.dma_start(aj_pl[:], aj_pool)
         offsets = held.tile([P, N // 16], U16, name="offsets")
         nc.sync.dma_start(offsets[:], offs)
+        w_t = held.tile([P, MB * P], BF16)
+        nc.sync.dma_start(w_t[:], w_conv)
         aj_cv = held.tile([P, MB, N], F32)
         nc.sync.dma_start(aj_cv[:], aj_conv.rearrange("(b p) j -> p b j", p=P))
 
@@ -93,11 +93,11 @@ def tile_lrpdensenettransition_kernel(
                 nc.vector.tensor_tensor(s_total[:], s_total[:], summand, ALU.add)
 
         mag_pl = held.tile([P, S], F32)
-        magnitude(nc, mag_pl[:], a_pl[:])
+        nc.scalar.activation(mag_pl[:], a_pl[:], ACT.Abs)
         inv_pl = held.tile([P, S], F32)
         inverse_of_stabilised(nc, inv_pl[:], mag_pl[:])
         share = held.tile([P, S], F32)
-        nc.vector.tensor_tensor(share[:], mag_pl[:], inv_pl[:], ALU.mult)
+        nc.scalar.activation(share[:], inv_pl[:], ACT.Identity, bias=1.0, scale=-E)
         s_pool = held.tile([P, S], F32)
         nc.vector.tensor_tensor(s_pool[:], s_total[:], share[:], ALU.mult)
 

@@ -75,22 +75,25 @@ def tile_lrpdensenettransition_kernel(
         wbn2 = held.tile([P, K], F32)
         nc.vector.scalar_tensor_tensor(wbn2[:], gamma_t[:], 2.0, rstd[:], ALU.mult, ALU.mult)
 
+
         mag_st = held.tile([P, K, S], F32)
         inv_st = held.tile([P, K, S], F32)
         sgn_st = held.tile([P, K, S], F32)
         term = held.tile([P, K, S], F32)
-        s_total = held.tile([P, S], F32)
         for k in range(K):
             magnitude(nc, mag_st[:, k, :], a_st[:, k, :])
-            inverse_of_stabilised(nc, inv_st[:, k, :], mag_st[:, k, :])
+        for k in range(K):
             half_sign(nc, sgn_st[:, k, :], a_st[:, k, :])
+        for k in range(K):
+            nc.scalar.activation(inv_st[:, k, :], mag_st[:, k, :], ACT.Abs_reciprocal_sqrt, bias=E)
+        for k in range(K):
+            nc.scalar.activation(inv_st[:, k, :], inv_st[:, k, :], ACT.Square)
+        for k in range(K):
             nc.vector.scalar_tensor_tensor(
                 term[:, k, :], r_st[:, k, :], wbn2[:, k : k + 1], sgn_st[:, k, :], ALU.mult, ALU.mult
             )
-            summand = s_total[:] if k == 0 else term[:, k, :]
-            nc.vector.tensor_tensor(summand, term[:, k, :], inv_st[:, k, :], ALU.mult)
-            if k > 0:
-                nc.vector.tensor_tensor(s_total[:], s_total[:], summand, ALU.add)
+        for k in range(K):
+            nc.vector.tensor_tensor(term[:, k, :], term[:, k, :], inv_st[:, k, :], ALU.mult)
 
         mag_pl = held.tile([P, S], F32)
         nc.scalar.activation(mag_pl[:], a_pl[:], ACT.Abs)
@@ -98,37 +101,67 @@ def tile_lrpdensenettransition_kernel(
         inverse_of_stabilised(nc, inv_pl[:], mag_pl[:])
         share = held.tile([P, S], F32)
         nc.scalar.activation(share[:], inv_pl[:], ACT.Identity, bias=1.0, scale=-E)
-        s_pool = held.tile([P, S], F32)
-        nc.vector.tensor_tensor(s_pool[:], s_total[:], share[:], ALU.mult)
 
         sgn_cv = held.tile([P, N], F32)
-        aj_signed = held.tile([P, N], F32)
         for i in range(NPIECES):
             cols = slice(i * PIECE, (i + 1) * PIECE)
             sign_of_stabilised(nc, sgn_cv[:, cols], a_cv[:, cols])
+
+        aj_signed = held.tile([P, N], F32)
+
+        def sign_aj_pool(i):
+            cols = slice(i * PIECE, (i + 1) * PIECE)
             nc.vector.tensor_tensor(aj_signed[:, cols], aj_pl[:, cols], sgn_cv[:, cols], ALU.mult)
+
+        sum_01 = held.tile([P, S], F32)
+        nc.vector.tensor_tensor(sum_01[:], term[:, 0, :], term[:, 1, :], ALU.add)
+        sum_23 = held.tile([P, S], F32)
+        nc.vector.tensor_tensor(sum_23[:], term[:, 2, :], term[:, 3, :], ALU.add)
+        sign_aj_pool(0)
+        s_total = held.tile([P, S], F32)
+        nc.vector.tensor_tensor(s_total[:], sum_01[:], sum_23[:], ALU.add)
+        sign_aj_pool(1)
+        s_pool = held.tile([P, S], F32)
+        nc.vector.tensor_tensor(s_pool[:], s_total[:], share[:], ALU.mult)
+        sign_aj_pool(2)
+        sign_aj_pool(3)
 
         mag_cv = held.tile([P, N], F32)
         inv_cv = held.tile([P, N], F32)
+        for first in range(0, NPIECES, 2):
+            both = [slice(i * PIECE, (i + 1) * PIECE) for i in (first, first + 1)]
+            for cols in both:
+                nc.scalar.activation(mag_cv[:, cols], a_cv[:, cols], ACT.Abs)
+            for cols in both:
+                nc.scalar.activation(inv_cv[:, cols], mag_cv[:, cols], ACT.Abs_reciprocal_sqrt, bias=E)
+            for cols in both:
+                nc.scalar.activation(inv_cv[:, cols], inv_cv[:, cols], ACT.Square)
+
         picked = held.tile([P, N], F32)
         sc = held.tile([P, N], BF16)
         result = held.tile([P, MB, N], F32)
         out_blocks = out.rearrange("(b p) j -> p b j", p=P)
-        for i in range(NPIECES):
-            cols = slice(i * PIECE, (i + 1) * PIECE)
-            nc.scalar.activation(mag_cv[:, cols], a_cv[:, cols], ACT.Abs)
-            inverse_of_stabilised(nc, inv_cv[:, cols], mag_cv[:, cols])
-            nc.vector.tensor_tensor(
-                picked[:, cols],
-                s_pool[:].indirect(offsets[:, i * (PIECE // 16) : (i + 1) * (PIECE // 16)]),
-                aj_signed[:, cols],
-                ALU.mult,
-            )
-            nc.vector.scalar_tensor_tensor(
-                sc[:, cols], picked[:, cols], POOL, inv_cv[:, cols], ALU.mult, ALU.mult
-            )
-            conv = psum_conv.tile([P, MB, PIECE], F32)
-            for b in range(MB):
-                nc.tensor.matmul(conv[:, b, :], w_t[:, b * P : (b + 1) * P], sc[:, cols], start=True, stop=True)
-            nc.vector.tensor_tensor(result[:, :, cols], conv[:], aj_cv[:, :, cols], ALU.mult)
-            nc.sync.dma_start(out_blocks[:, :, cols], result[:, :, cols])
+        convs = []
+        for step in range(NPIECES + 2):
+            if step < NPIECES:
+                i = step
+                cols = slice(i * PIECE, (i + 1) * PIECE)
+                nc.vector.tensor_tensor(
+                    picked[:, cols],
+                    s_pool[:].indirect(offsets[:, i * (PIECE // 16) : (i + 1) * (PIECE // 16)]),
+                    aj_signed[:, cols],
+                    ALU.mult,
+                )
+            if 1 <= step <= NPIECES:
+                cols = slice((step - 1) * PIECE, step * PIECE)
+                nc.vector.scalar_tensor_tensor(
+                    sc[:, cols], picked[:, cols], POOL, inv_cv[:, cols], ALU.mult, ALU.mult
+                )
+                conv = psum_conv.tile([P, MB, PIECE], F32)
+                for b in range(MB):
+                    nc.tensor.matmul(conv[:, b, :], w_t[:, b * P : (b + 1) * P], sc[:, cols], start=True, stop=True)
+                convs.append(conv)
+            if step >= 2:
+                cols = slice((step - 2) * PIECE, (step - 1) * PIECE)
+                nc.vector.tensor_tensor(result[:, :, cols], convs[step - 2][:], aj_cv[:, :, cols], ALU.mult)
+                nc.sync.dma_start(out_blocks[:, :, cols], result[:, :, cols])

@@ -26,11 +26,6 @@ def magnitude(nc, out, z):
     nc.vector.tensor_scalar(out.bitcast(I32), z.bitcast(I32), ALL_BUT_SIGN, None, ALU.bitwise_and)
 
 
-def inverse_of_stabilised(nc, out, mag):
-    nc.scalar.activation(out, mag, ACT.Abs_reciprocal_sqrt, bias=E)
-    nc.scalar.activation(out, out, ACT.Square)
-
-
 def half_sign(nc, out, z):
     nc.vector.tensor_scalar(out, z, 0.0, 0.5, ALU.is_ge, ALU.subtract)
 
@@ -96,16 +91,22 @@ def tile_lrpdensenettransition_kernel(
             nc.vector.tensor_tensor(term[:, k, :], term[:, k, :], inv_st[:, k, :], ALU.mult)
 
         mag_pl = held.tile([P, S], F32)
-        nc.scalar.activation(mag_pl[:], a_pl[:], ACT.Abs)
         inv_pl = held.tile([P, S], F32)
-        inverse_of_stabilised(nc, inv_pl[:], mag_pl[:])
         share = held.tile([P, S], F32)
-        nc.scalar.activation(share[:], inv_pl[:], ACT.Identity, bias=1.0, scale=-E)
-
         sgn_cv = held.tile([P, N], F32)
-        for i in range(NPIECES):
+
+        def sign_of_piece(i):
             cols = slice(i * PIECE, (i + 1) * PIECE)
             sign_of_stabilised(nc, sgn_cv[:, cols], a_cv[:, cols])
+
+        nc.scalar.activation(mag_pl[:], a_pl[:], ACT.Abs)
+        sign_of_piece(0)
+        nc.scalar.activation(inv_pl[:], mag_pl[:], ACT.Abs_reciprocal_sqrt, bias=E)
+        sign_of_piece(1)
+        nc.scalar.activation(inv_pl[:], inv_pl[:], ACT.Square)
+        sign_of_piece(2)
+        nc.scalar.activation(share[:], inv_pl[:], ACT.Identity, bias=1.0, scale=-E)
+        sign_of_piece(3)
 
         aj_signed = held.tile([P, N], F32)
 
@@ -142,13 +143,12 @@ def tile_lrpdensenettransition_kernel(
         result = held.tile([P, MB, N], F32)
         out_blocks = out.rearrange("(b p) j -> p b j", p=P)
         convs = []
-        for step in range(NPIECES + 2):
+        for step in range(NPIECES + 3):
             if step < NPIECES:
-                i = step
-                cols = slice(i * PIECE, (i + 1) * PIECE)
+                cols = slice(step * PIECE, (step + 1) * PIECE)
                 nc.vector.tensor_tensor(
                     picked[:, cols],
-                    s_pool[:].indirect(offsets[:, i * (PIECE // 16) : (i + 1) * (PIECE // 16)]),
+                    s_pool[:].indirect(offsets[:, step * (PIECE // 16) : (step + 1) * (PIECE // 16)]),
                     aj_signed[:, cols],
                     ALU.mult,
                 )
@@ -161,7 +161,7 @@ def tile_lrpdensenettransition_kernel(
                 for b in range(MB):
                     nc.tensor.matmul(conv[:, b, :], w_t[:, b * P : (b + 1) * P], sc[:, cols], start=True, stop=True)
                 convs.append(conv)
-            if step >= 2:
-                cols = slice((step - 2) * PIECE, (step - 1) * PIECE)
-                nc.vector.tensor_tensor(result[:, :, cols], convs[step - 2][:], aj_cv[:, :, cols], ALU.mult)
+            if step >= 3:
+                cols = slice((step - 3) * PIECE, (step - 2) * PIECE)
+                nc.vector.tensor_tensor(result[:, :, cols], convs[step - 3][:], aj_cv[:, :, cols], ALU.mult)
                 nc.sync.dma_start(out_blocks[:, :, cols], result[:, :, cols])

@@ -136,14 +136,14 @@ def tile_lrpdensenettransition_kernel(
             for cols in both:
                 nc.scalar.activation(inv_cv[:, cols], mag_cv[:, cols], ACT.Abs_reciprocal_sqrt, bias=E)
             for cols in both:
-                nc.scalar.activation(inv_cv[:, cols], inv_cv[:, cols], ACT.Square)
+                nc.scalar.activation(inv_cv[:, cols], inv_cv[:, cols], ACT.Square, scale=POOL**0.5)
 
         picked = held.tile([P, N], F32)
         sc = held.tile([P, N], BF16)
         result = held.tile([P, MB, N], F32)
         out_blocks = out.rearrange("(b p) j -> p b j", p=P)
         convs = []
-        for step in range(NPIECES + 3):
+        for step in range(NPIECES + 2):
             if step < NPIECES:
                 cols = slice(step * PIECE, (step + 1) * PIECE)
                 nc.vector.tensor_tensor(
@@ -154,14 +154,13 @@ def tile_lrpdensenettransition_kernel(
                 )
             if 1 <= step <= NPIECES:
                 cols = slice((step - 1) * PIECE, step * PIECE)
-                nc.vector.scalar_tensor_tensor(
-                    sc[:, cols], picked[:, cols], POOL, inv_cv[:, cols], ALU.mult, ALU.mult
-                )
+                scaler = nc.vector if step - 1 < 2 else nc.gpsimd
+                scaler.tensor_tensor(sc[:, cols], picked[:, cols], inv_cv[:, cols], ALU.mult)
                 conv = psum_conv.tile([P, MB, PIECE], F32)
                 for b in range(MB):
                     nc.tensor.matmul(conv[:, b, :], w_t[:, b * P : (b + 1) * P], sc[:, cols], start=True, stop=True)
                 convs.append(conv)
-            if step >= 3:
-                cols = slice((step - 3) * PIECE, (step - 2) * PIECE)
-                nc.vector.tensor_tensor(result[:, :, cols], convs[step - 3][:], aj_cv[:, :, cols], ALU.mult)
+            if step >= 2:
+                cols = slice((step - 2) * PIECE, (step - 1) * PIECE)
+                nc.vector.tensor_tensor(result[:, :, cols], convs[step - 2][:], aj_cv[:, :, cols], ALU.mult)
                 nc.sync.dma_start(out_blocks[:, :, cols], result[:, :, cols])

@@ -75,7 +75,9 @@ def tile_lrpdensenettransition_kernel(
         inv_st = held.tile([P, K, S], F32)
         sgn_st = held.tile([P, K, S], F32)
         term = held.tile([P, K, S], F32)
-        for k in range(K):
+        for k in range(2):
+            nc.scalar.activation(mag_st[:, k, :], a_st[:, k, :], ACT.Abs)
+        for k in range(2, K):
             magnitude(nc, mag_st[:, k, :], a_st[:, k, :])
         for k in range(K):
             half_sign(nc, sgn_st[:, k, :], a_st[:, k, :])

@@ -83,62 +83,67 @@ def tile_lrpdensenettransition_kernel(
             half_sign(nc, sgn_st[:, k, :], a_st[:, k, :])
         for k in range(K):
             nc.scalar.activation(inv_st[:, k, :], mag_st[:, k, :], ACT.Abs_reciprocal_sqrt, bias=E)
-        for k in range(K):
+        mag_pl = held.tile([P, S], F32)
+        inv_pl = held.tile([P, S], F32)
+        for k in range(K - 1):
             nc.scalar.activation(inv_st[:, k, :], inv_st[:, k, :], ACT.Square)
+        nc.scalar.activation(mag_pl[:], a_pl[:], ACT.Abs)
+        nc.scalar.activation(inv_st[:, K - 1, :], inv_st[:, K - 1, :], ACT.Square)
+        nc.scalar.activation(inv_pl[:], mag_pl[:], ACT.Abs_reciprocal_sqrt, bias=E)
         for k in range(K):
             nc.vector.scalar_tensor_tensor(
                 term[:, k, :], r_st[:, k, :], wbn2[:, k : k + 1], sgn_st[:, k, :], ALU.mult, ALU.mult
             )
-        for k in range(K):
+        mag_cv = held.tile([P, N], F32)
+
+        def invert_term(k):
             nc.vector.tensor_tensor(term[:, k, :], term[:, k, :], inv_st[:, k, :], ALU.mult)
 
-        mag_pl = held.tile([P, S], F32)
-        inv_pl = held.tile([P, S], F32)
+        for k in range(3):
+            invert_term(k)
+        sum_01 = held.tile([P, S], F32)
+        nc.vector.tensor_tensor(sum_01[:], term[:, 0, :], term[:, 1, :], ALU.add)
+        invert_term(3)
+        sum_012 = held.tile([P, S], F32)
+        nc.vector.tensor_tensor(sum_012[:], sum_01[:], term[:, 2, :], ALU.add)
+        magnitude(nc, mag_cv[:, N // 2 :], a_cv[:, N // 2 :])
+        s_total = held.tile([P, S], F32)
+        nc.vector.tensor_tensor(s_total[:], sum_012[:], term[:, 3, :], ALU.add)
+
         share = held.tile([P, S], F32)
         sgn_cv = held.tile([P, N], F32)
+        inv_cv = held.tile([P, N], F32)
+        pieces = [slice(i * PIECE, (i + 1) * PIECE) for i in range(NPIECES)]
 
         def sign_of_piece(i):
-            cols = slice(i * PIECE, (i + 1) * PIECE)
-            sign_of_stabilised(nc, sgn_cv[:, cols], a_cv[:, cols])
+            sign_of_stabilised(nc, sgn_cv[:, pieces[i]], a_cv[:, pieces[i]])
 
-        nc.scalar.activation(mag_pl[:], a_pl[:], ACT.Abs)
-        sign_of_piece(0)
-        nc.scalar.activation(inv_pl[:], mag_pl[:], ACT.Abs_reciprocal_sqrt, bias=E)
-        sign_of_piece(1)
+        def inverse_of_pair(pair):
+            for cols in pair:
+                nc.scalar.activation(inv_cv[:, cols], mag_cv[:, cols], ACT.Abs_reciprocal_sqrt, bias=E)
+            for cols in pair:
+                nc.scalar.activation(inv_cv[:, cols], inv_cv[:, cols], ACT.Square, scale=POOL**0.5)
+
         nc.scalar.activation(inv_pl[:], inv_pl[:], ACT.Square)
-        sign_of_piece(2)
+        sign_of_piece(0)
         nc.scalar.activation(share[:], inv_pl[:], ACT.Identity, bias=1.0, scale=-E)
-        sign_of_piece(3)
+        for i in range(1, NPIECES):
+            sign_of_piece(i)
+        for cols in pieces[:2]:
+            nc.scalar.activation(mag_cv[:, cols], a_cv[:, cols], ACT.Abs)
+        inverse_of_pair(pieces[:2])
+        inverse_of_pair(pieces[2:])
 
         aj_signed = held.tile([P, N], F32)
 
         def sign_aj_pool(i):
-            cols = slice(i * PIECE, (i + 1) * PIECE)
-            nc.vector.tensor_tensor(aj_signed[:, cols], aj_pl[:, cols], sgn_cv[:, cols], ALU.mult)
+            nc.vector.tensor_tensor(aj_signed[:, pieces[i]], aj_pl[:, pieces[i]], sgn_cv[:, pieces[i]], ALU.mult)
 
-        sum_01 = held.tile([P, S], F32)
-        nc.vector.tensor_tensor(sum_01[:], term[:, 0, :], term[:, 1, :], ALU.add)
-        sum_23 = held.tile([P, S], F32)
-        nc.vector.tensor_tensor(sum_23[:], term[:, 2, :], term[:, 3, :], ALU.add)
         sign_aj_pool(0)
-        s_total = held.tile([P, S], F32)
-        nc.vector.tensor_tensor(s_total[:], sum_01[:], sum_23[:], ALU.add)
-        sign_aj_pool(1)
         s_pool = held.tile([P, S], F32)
         nc.vector.tensor_tensor(s_pool[:], s_total[:], share[:], ALU.mult)
-        sign_aj_pool(2)
-        sign_aj_pool(3)
-
-        mag_cv = held.tile([P, N], F32)
-        inv_cv = held.tile([P, N], F32)
-        for first in range(0, NPIECES, 2):
-            both = [slice(i * PIECE, (i + 1) * PIECE) for i in (first, first + 1)]
-            for cols in both:
-                nc.scalar.activation(mag_cv[:, cols], a_cv[:, cols], ACT.Abs)
-            for cols in both:
-                nc.scalar.activation(inv_cv[:, cols], mag_cv[:, cols], ACT.Abs_reciprocal_sqrt, bias=E)
-            for cols in both:
-                nc.scalar.activation(inv_cv[:, cols], inv_cv[:, cols], ACT.Square, scale=POOL**0.5)
+        for i in range(1, NPIECES):
+            sign_aj_pool(i)
 
         picked = held.tile([P, N], F32)
         sc = held.tile([P, N], BF16)
@@ -147,7 +152,7 @@ def tile_lrpdensenettransition_kernel(
         convs = []
         for step in range(NPIECES + 2):
             if step < NPIECES:
-                cols = slice(step * PIECE, (step + 1) * PIECE)
+                cols = pieces[step]
                 nc.vector.tensor_tensor(
                     picked[:, cols],
                     s_pool[:].indirect(offsets[:, step * (PIECE // 16) : (step + 1) * (PIECE // 16)]),
@@ -155,7 +160,7 @@ def tile_lrpdensenettransition_kernel(
                     ALU.mult,
                 )
             if 1 <= step <= NPIECES:
-                cols = slice((step - 1) * PIECE, step * PIECE)
+                cols = pieces[step - 1]
                 scaler = nc.vector if step - 1 < 2 else nc.gpsimd
                 scaler.tensor_tensor(sc[:, cols], picked[:, cols], inv_cv[:, cols], ALU.mult)
                 conv = psum_conv.tile([P, MB, PIECE], F32)
@@ -163,6 +168,6 @@ def tile_lrpdensenettransition_kernel(
                     nc.tensor.matmul(conv[:, b, :], w_t[:, b * P : (b + 1) * P], sc[:, cols], start=True, stop=True)
                 convs.append(conv)
             if step >= 2:
-                cols = slice((step - 2) * PIECE, (step - 1) * PIECE)
+                cols = pieces[step - 2]
                 nc.vector.tensor_tensor(result[:, :, cols], convs[step - 2][:], aj_cv[:, :, cols], ALU.mult)
                 nc.sync.dma_start(out_blocks[:, :, cols], result[:, :, cols])

@@ -106,17 +106,16 @@ def tile_lrpdensenettransition_kernel(
         invert_term(3)
         sum_012 = held.tile([P, S], F32)
         nc.vector.tensor_tensor(sum_012[:], sum_01[:], term[:, 2, :], ALU.add)
-        magnitude(nc, mag_cv[:, N // 2 :], a_cv[:, N // 2 :])
+        magnitude(nc, mag_cv[:, : N // 2], a_cv[:, : N // 2])
         s_total = held.tile([P, S], F32)
         nc.vector.tensor_tensor(s_total[:], sum_012[:], term[:, 3, :], ALU.add)
 
         share = held.tile([P, S], F32)
-        sgn_cv = held.tile([P, N], F32)
         inv_cv = held.tile([P, N], F32)
+        sgn_first = held.tile([P, N // 2], BF16)
+        sgn_second = held.tile([P, N // 2], F32)
         pieces = [slice(i * PIECE, (i + 1) * PIECE) for i in range(NPIECES)]
-
-        def sign_of_piece(i):
-            sign_of_stabilised(nc, sgn_cv[:, pieces[i]], a_cv[:, pieces[i]])
+        in_half = [pieces[i % 2] for i in range(NPIECES)]
 
         def inverse_of_pair(pair):
             for cols in pair:
@@ -125,49 +124,65 @@ def tile_lrpdensenettransition_kernel(
                 nc.scalar.activation(inv_cv[:, cols], inv_cv[:, cols], ACT.Square, scale=POOL**0.5)
 
         nc.scalar.activation(inv_pl[:], inv_pl[:], ACT.Square)
-        sign_of_piece(0)
+        sign_of_stabilised(nc, sgn_second[:, in_half[2]], a_cv[:, pieces[2]])
         nc.scalar.activation(share[:], inv_pl[:], ACT.Identity, bias=1.0, scale=-E)
-        for i in range(1, NPIECES):
-            sign_of_piece(i)
-        for cols in pieces[:2]:
-            nc.scalar.activation(mag_cv[:, cols], a_cv[:, cols], ACT.Abs)
+        sign_of_stabilised(nc, sgn_second[:, in_half[3]], a_cv[:, pieces[3]])
         inverse_of_pair(pieces[:2])
+        for i in range(2):
+            sign_of_stabilised(nc, sgn_first[:, in_half[i]], a_cv[:, pieces[i]])
+        for cols in pieces[2:]:
+            nc.scalar.activation(mag_cv[:, cols], a_cv[:, cols], ACT.Abs)
         inverse_of_pair(pieces[2:])
 
-        aj_signed = held.tile([P, N], F32)
+        aj_signed = held.tile([P, N // 2], F32)
 
         def sign_aj_pool(i):
-            nc.vector.tensor_tensor(aj_signed[:, pieces[i]], aj_pl[:, pieces[i]], sgn_cv[:, pieces[i]], ALU.mult)
+            nc.vector.tensor_tensor(
+                aj_signed[:, in_half[i]], aj_pl[:, pieces[i]], sgn_second[:, in_half[i]], ALU.mult
+            )
 
-        sign_aj_pool(0)
+        sign_aj_pool(2)
         s_pool = held.tile([P, S], F32)
         nc.vector.tensor_tensor(s_pool[:], s_total[:], share[:], ALU.mult)
-        for i in range(1, NPIECES):
-            sign_aj_pool(i)
+        sign_aj_pool(3)
 
         picked = held.tile([P, N], F32)
+        unsigned = held.tile([P, N // 2], BF16)
         sc = held.tile([P, N], BF16)
         result = held.tile([P, MB, N], F32)
         out_blocks = out.rearrange("(b p) j -> p b j", p=P)
-        convs = []
-        for step in range(NPIECES + 2):
-            if step < NPIECES:
-                cols = pieces[step]
-                nc.vector.tensor_tensor(
-                    picked[:, cols],
-                    s_pool[:].indirect(offsets[:, step * (PIECE // 16) : (step + 1) * (PIECE // 16)]),
-                    aj_signed[:, cols],
-                    ALU.mult,
-                )
-            if 1 <= step <= NPIECES:
-                cols = pieces[step - 1]
-                scaler = nc.vector if step - 1 < 2 else nc.gpsimd
-                scaler.tensor_tensor(sc[:, cols], picked[:, cols], inv_cv[:, cols], ALU.mult)
-                conv = psum_conv.tile([P, MB, PIECE], F32)
-                for b in range(MB):
-                    nc.tensor.matmul(conv[:, b, :], w_t[:, b * P : (b + 1) * P], sc[:, cols], start=True, stop=True)
-                convs.append(conv)
-            if step >= 2:
-                cols = pieces[step - 2]
-                nc.vector.tensor_tensor(result[:, :, cols], convs[step - 2][:], aj_cv[:, :, cols], ALU.mult)
-                nc.sync.dma_start(out_blocks[:, :, cols], result[:, :, cols])
+
+        def look_up(i, weight):
+            entries = offsets[:, i * (PIECE // 16) : (i + 1) * (PIECE // 16)]
+            nc.vector.tensor_tensor(picked[:, pieces[i]], s_pool[:].indirect(entries), weight, ALU.mult)
+
+        def scale(engine, scaled, i):
+            engine.tensor_tensor(scaled, picked[:, pieces[i]], inv_cv[:, pieces[i]], ALU.mult)
+
+        def sign_scaled(i):
+            nc.vector.tensor_tensor(sc[:, pieces[i]], unsigned[:, in_half[i]], sgn_first[:, in_half[i]], ALU.mult)
+
+        def convolve(i):
+            conv = psum_conv.tile([P, MB, PIECE], F32)
+            for b in range(MB):
+                nc.tensor.matmul(conv[:, b, :], w_t[:, b * P : (b + 1) * P], sc[:, pieces[i]], start=True, stop=True)
+            return conv
+
+        def weigh_and_store(conv, i):
+            nc.vector.tensor_tensor(result[:, :, pieces[i]], conv[:], aj_cv[:, :, pieces[i]], ALU.mult)
+            nc.sync.dma_start(out_blocks[:, :, pieces[i]], result[:, :, pieces[i]])
+
+        look_up(0, aj_pl[:, pieces[0]])
+        look_up(1, aj_pl[:, pieces[1]])
+        scale(nc.vector, unsigned[:, in_half[0]], 0)
+        scale(nc.vector, unsigned[:, in_half[1]], 1)
+        sign_scaled(0)
+        sign_scaled(1)
+        convs = [convolve(0), convolve(1)]
+        look_up(2, aj_signed[:, in_half[2]])
+        look_up(3, aj_signed[:, in_half[3]])
+        scale(nc.vector, sc[:, pieces[2]], 2)
+        scale(nc.gpsimd, sc[:, pieces[3]], 3)
+        convs += [convolve(2), convolve(3)]
+        for i in range(NPIECES):
+            weigh_and_store(convs[i], i)

@@ -181,7 +181,7 @@ def tile_lrpdensenettransition_kernel(
         convs = [convolve(0), convolve(1)]
         look_up(2, aj_signed[:, in_half[2]])
         look_up(3, aj_signed[:, in_half[3]])
-        scale(nc.vector, sc[:, pieces[2]], 2)
+        scale(nc.gpsimd, sc[:, pieces[2]], 2)
         scale(nc.gpsimd, sc[:, pieces[3]], 3)
         convs += [convolve(2), convolve(3)]
         for i in range(NPIECES):

import concourse.mybir as mybir

F32 = mybir.dt.float32
BF16 = mybir.dt.bfloat16
I32 = mybir.dt.int32
U16 = mybir.dt.uint16
ALU = mybir.AluOpType
ACT = mybir.ActivationFunctionType

P = 128
K = 4
S = 256
N = 1024
MB = 2
PIECE = 256
NPIECES = N // PIECE
E = 0.01
BN_EPS = 1e-5
POOL = 0.25
ALL_BUT_SIGN = 0x7FFFFFFF

FLOPS = 2 * P * MB * P * N


def magnitude(nc, out, z):
    nc.vector.tensor_scalar(out.bitcast(I32), z.bitcast(I32), ALL_BUT_SIGN, None, ALU.bitwise_and)


def half_sign(nc, out, z):
    nc.vector.tensor_scalar(out, z, 0.0, 0.5, ALU.is_ge, ALU.subtract)


def sign_of_stabilised(nc, out, z):
    nc.scalar.activation(out, z, ACT.Sign, bias=2.0**-126, scale=2.0**24)


def tile_lrpdensenettransition_kernel(
    tc, r_stack, a_stack, gamma, var, a_pool, aj_pool, a_conv, aj_conv, w_conv, offs, out
):
    nc = tc.nc
    with (
        tc.tile_pool(name="held", bufs=1) as held,
        tc.psum_pool(name="psum_conv", bufs=NPIECES) as psum_conv,
    ):
        var_t = held.tile([P, K], F32)
        nc.sync.dma_start(var_t[:], var)
        gamma_t = held.tile([P, K], F32)
        nc.sync.dma_start(gamma_t[:], gamma)
        a_st = held.tile([P, K, S], F32)
        for k in range(0, K, 2):
            nc.sync.dma_start(a_st[:, k : k + 2, :], a_stack[k : k + 2].rearrange("k c s -> c k s"))
        r_st = held.tile([P, K, S], F32)
        for k in range(0, K, 2):
            nc.sync.dma_start(r_st[:, k : k + 2, :], r_stack[k : k + 2].rearrange("k c s -> c k s"))
        a_pl = held.tile([P, S], F32)
        nc.sync.dma_start(a_pl[:], a_pool)
        a_cv = held.tile([P, N], F32)
        nc.sync.dma_start(a_cv[:], a_conv)
        aj_pl = held.tile([P, N], F32)
        nc.sync.dma_start(aj_pl[:], aj_pool)
        offsets = held.tile([P, N // 16], U16, name="offsets")
        nc.sync.dma_start(offsets[:], offs)
        w_t = held.tile([P, MB * P], BF16)
        nc.sync.dma_start(w_t[:], w_conv)
        aj_cv = held.tile([P, MB, N], F32)
        nc.sync.dma_start(aj_cv[:], aj_conv.rearrange("(b p) j -> p b j", p=P))

        rstd = held.tile([P, K], F32)
        nc.scalar.activation(rstd[:], var_t[:], ACT.Abs_reciprocal_sqrt, bias=BN_EPS)
        wbn2 = held.tile([P, K], F32)
        nc.vector.scalar_tensor_tensor(wbn2[:], gamma_t[:], 2.0, rstd[:], ALU.mult, ALU.mult)


        mag_st = held.tile([P, K, S], F32)
        inv_st = held.tile([P, K, S], F32)
        sgn_st = held.tile([P, K, S], F32)
        term = held.tile([P, K, S], F32)
        for k in range(2):
            nc.scalar.activation(mag_st[:, k, :], a_st[:, k, :], ACT.Abs)
        for k in range(2, K):
            magnitude(nc, mag_st[:, k, :], a_st[:, k, :])
        for k in range(K):
            half_sign(nc, sgn_st[:, k, :], a_st[:, k, :])
        for k in range(K):
            nc.scalar.activation(inv_st[:, k, :], mag_st[:, k, :], ACT.Abs_reciprocal_sqrt, bias=E)
        mag_pl = held.tile([P, S], F32)
        inv_pl = held.tile([P, S], F32)
        for k in range(K - 1):
            nc.scalar.activation(inv_st[:, k, :], inv_st[:, k, :], ACT.Square)
        nc.scalar.activation(mag_pl[:], a_pl[:], ACT.Abs)
        nc.scalar.activation(inv_st[:, K - 1, :], inv_st[:, K - 1, :], ACT.Square)
        nc.scalar.activation(inv_pl[:], mag_pl[:], ACT.Abs_reciprocal_sqrt, bias=E)
        for k in range(K):
            nc.vector.scalar_tensor_tensor(
                term[:, k, :], r_st[:, k, :], wbn2[:, k : k + 1], sgn_st[:, k, :], ALU.mult, ALU.mult
            )
        mag_cv = held.tile([P, N], F32)

        def invert_term(k):
            nc.vector.tensor_tensor(term[:, k, :], term[:, k, :], inv_st[:, k, :], ALU.mult)

        for k in range(3):
            invert_term(k)
        sum_01 = held.tile([P, S], F32)
        nc.vector.tensor_tensor(sum_01[:], term[:, 0, :], term[:, 1, :], ALU.add)
        invert_term(3)
        sum_012 = held.tile([P, S], F32)
        nc.vector.tensor_tensor(sum_012[:], sum_01[:], term[:, 2, :], ALU.add)
        magnitude(nc, mag_cv[:, : N // 2], a_cv[:, : N // 2])
        s_total = held.tile([P, S], F32)
        nc.vector.tensor_tensor(s_total[:], sum_012[:], term[:, 3, :], ALU.add)

        share = held.tile([P, S], F32)
        inv_cv = held.tile([P, N], F32)
        sgn_first = held.tile([P, N // 2], BF16)
        sgn_second = held.tile([P, N // 2], F32)
        pieces = [slice(i * PIECE, (i + 1) * PIECE) for i in range(NPIECES)]
        in_half = [pieces[i % 2] for i in range(NPIECES)]

        def inverse_of_pair(pair):
            for cols in pair:
                nc.scalar.activation(inv_cv[:, cols], mag_cv[:, cols], ACT.Abs_reciprocal_sqrt, bias=E)
            for cols in pair:
                nc.scalar.activation(inv_cv[:, cols], inv_cv[:, cols], ACT.Square, scale=POOL**0.5)

        nc.scalar.activation(inv_pl[:], inv_pl[:], ACT.Square)
        sign_of_stabilised(nc, sgn_second[:, in_half[2]], a_cv[:, pieces[2]])
        nc.scalar.activation(share[:], inv_pl[:], ACT.Identity, bias=1.0, scale=-E)
        sign_of_stabilised(nc, sgn_second[:, in_half[3]], a_cv[:, pieces[3]])
        inverse_of_pair(pieces[:2])
        for i in range(2):
            sign_of_stabilised(nc, sgn_first[:, in_half[i]], a_cv[:, pieces[i]])
        for cols in pieces[2:]:
            nc.scalar.activation(mag_cv[:, cols], a_cv[:, cols], ACT.Abs)
        inverse_of_pair(pieces[2:])

        aj_signed = held.tile([P, N // 2], F32)

        def sign_aj_pool(i):
            nc.vector.tensor_tensor(
                aj_signed[:, in_half[i]], aj_pl[:, pieces[i]], sgn_second[:, in_half[i]], ALU.mult
            )

        sign_aj_pool(2)
        s_pool = held.tile([P, S], F32)
        nc.vector.tensor_tensor(s_pool[:], s_total[:], share[:], ALU.mult)
        sign_aj_pool(3)

        picked = held.tile([P, N], F32)
        unsigned = held.tile([P, N // 2], BF16)
        sc = held.tile([P, N], BF16)
        result = held.tile([P, MB, N], F32)
        out_blocks = out.rearrange("(b p) j -> p b j", p=P)

        def look_up(i, weight):
            entries = offsets[:, i * (PIECE // 16) : (i + 1) * (PIECE // 16)]
            nc.vector.tensor_tensor(picked[:, pieces[i]], s_pool[:].indirect(entries), weight, ALU.mult)

        def scale(engine, scaled, i):
            engine.tensor_tensor(scaled, picked[:, pieces[i]], inv_cv[:, pieces[i]], ALU.mult)

        def sign_scaled(i):
            nc.vector.tensor_tensor(sc[:, pieces[i]], unsigned[:, in_half[i]], sgn_first[:, in_half[i]], ALU.mult)

        def convolve(i):
            conv = psum_conv.tile([P, MB, PIECE], F32)
            for b in range(MB):
                nc.tensor.matmul(conv[:, b, :], w_t[:, b * P : (b + 1) * P], sc[:, pieces[i]], start=True, stop=True)
            return conv

        def weigh_and_store(conv, i):
            nc.vector.tensor_tensor(result[:, :, pieces[i]], conv[:], aj_cv[:, :, pieces[i]], ALU.mult)
            nc.sync.dma_start(out_blocks[:, :, pieces[i]], result[:, :, pieces[i]])

        look_up(0, aj_pl[:, pieces[0]])
        look_up(1, aj_pl[:, pieces[1]])
        scale(nc.vector, unsigned[:, in_half[0]], 0)
        scale(nc.vector, unsigned[:, in_half[1]], 1)
        sign_scaled(0)
        sign_scaled(1)
        convs = [convolve(0), convolve(1)]
        look_up(2, aj_signed[:, in_half[2]])
        look_up(3, aj_signed[:, in_half[3]])
        scale(nc.gpsimd, sc[:, pieces[2]], 2)
        scale(nc.gpsimd, sc[:, pieces[3]], 3)
        convs += [convolve(2), convolve(3)]
        for i in range(NPIECES):
            weigh_and_store(convs[i], i)
